import numpy as np
import ml_dtypes


def mxq(x, axis, fmt="e4m3"):
    dtype, down = {"e4m3": (ml_dtypes.float8_e4m3fn, 7), "e5m2": (ml_dtypes.float8_e5m2, 14)}[fmt]
    v = np.moveaxis(np.asarray(x, np.float32).astype(ml_dtypes.bfloat16).astype(np.float64), axis, -1)
    blocks = v.reshape(v.shape[:-1] + (-1, 32))
    amax = np.abs(blocks).max(-1, keepdims=True)
    byte = np.maximum(np.where(amax > 0, np.frexp(amax)[1] - 1 + 127, 0) - down, 1)
    scale = np.exp2(byte - 127.0)
    codes = (blocks / scale).astype(np.float32).astype(dtype).astype(np.float64)
    return np.moveaxis((codes * scale).reshape(v.shape), -1, axis)


WIDE = False


def mx_kscale(k):
    if not WIDE:
        return np.ones(k)
    levels = np.array([10, -10, 5, -5, 0])
    if k % 512:
        return np.exp2(np.random.permutation(np.resize(levels, k // 32))).repeat(32)
    a = np.empty((k // 512, 16))
    for p in range(k // 512):
        a[p, :8] = np.random.permutation(np.resize(levels, 8))
        for g in range(8):
            far = levels[np.abs(levels - a[p, g]) >= 10]
            a[p, g + 8] = far[np.random.randint(len(far))]
    return np.exp2(a.ravel()).repeat(32)


BF16 = ml_dtypes.bfloat16


def bf(x):
    return np.asarray(x, np.float32).astype(BF16)


def f64(x):
    return np.asarray(x).astype(np.float64)


B, S, DIM, H, HD = 4, 128, 2048, 16, 128
E = H * HD


def rope_tables():
    inv_freq = 1.0 / (10000.0 ** (np.arange(0, HD, 2) / HD))
    freqs = np.outer(np.arange(S), inv_freq)
    emb = np.concatenate([freqs, freqs], axis=-1)
    return np.cos(emb)[None, None], np.sin(emb)[None, None]


def rotate_half(x):
    x1, x2 = np.split(x, 2, axis=-1)
    return np.concatenate([-x2, x1], axis=-1)


def setup_inputs():
    s = mx_kscale(DIM)
    cos, sin = rope_tables()
    return {"key_value": bf(np.random.standard_normal((B, S, DIM)) * s),
            "wk": bf(np.random.standard_normal((E, DIM)) / np.sqrt(DIM) / s),
            "bk": bf(np.random.standard_normal(E) * 0.1),
            "wv": bf(np.random.standard_normal((E, DIM)) / np.sqrt(DIM) / s),
            "bv": bf(np.random.standard_normal(E) * 0.1),
            "cos": bf(cos), "sin": bf(sin)}


def reference(key_value, wk, bk, wv, bv, cos, sin):
    xq = mxq(f64(key_value), 2, "e4m3")
    k = (xq @ mxq(f64(wk), 1, "e4m3").T) + f64(bk)
    v = (xq @ mxq(f64(wv), 1, "e4m3").T) + f64(bv)
    k = k.reshape(B, S, H, HD).transpose(0, 2, 1, 3)
    v = v.reshape(B, S, H, HD).transpose(0, 2, 1, 3)
    k = k * f64(cos) + rotate_half(k) * f64(sin)
    return k, v

@@ -1,0 +1,297 @@
+from contextlib import ExitStack
+
+import concourse.mybir as mybir
+from concourse.masks import make_identity
+
+F32 = mybir.dt.float32
+BF16 = mybir.dt.bfloat16
+U32 = mybir.dt.uint32
+U8 = mybir.dt.uint8
+I32 = mybir.dt.int32
+FP8X4 = mybir.dt.float8_e4m3fn_x4
+ADD = mybir.AluOpType.add
+MULT = mybir.AluOpType.mult
+
+P = 128
+B, S, DIM, H, HD = 4, 128, 2048, 16, 128
+FLOPS = 2 * B * S * DIM * 2 * H * HD
+
+SIN_ON_GPSIMD = False
+DEFER_A = 2
+DEFER_B = 1
+CHUNKS = [(True, 0), (False, 0), (True, 1), (False, 1), (True, 2), (False, 2), (True, 3), (False, 3)]
+LAST = len(CHUNKS) - 1
+
+
+def tile_attention_pb_kernel(tc, key_value, wk, bk, wv, bv, cos, sin, out_0, out_1):
+    nc = tc.nc
+    with ExitStack() as ctx:
+        const = ctx.enter_context(tc.tile_pool(name="const", bufs=1))
+        rawp = ctx.enter_context(tc.tile_pool(name="rawp", bufs=6))
+        grp = ctx.enter_context(tc.tile_pool(name="grp", bufs=6))
+        wqp = ctx.enter_context(tc.tile_pool(name="wqp", bufs=2))
+        outp = ctx.enter_context(tc.tile_pool(name="outp", bufs=12))
+        tmpp = ctx.enter_context(tc.tile_pool(name="tmpp", bufs=4))
+        tps = ctx.enter_context(tc.psum_pool(name="tps", bufs=4))
+        accp = ctx.enter_context(tc.psum_pool(name="accp", bufs=4))
+        ctx.enter_context(tc.manual_schedule())
+
+        raws = {}
+
+        def load_x():
+            raw = rawp.tile([P, 4 * DIM], BF16, name="raw", tag="raw")
+            for b in range(B):
+                nc.sync.dma_start(out=raw[:, b * DIM:(b + 1) * DIM], in_=key_value[b])
+            raws["x"] = raw[:].bitcast(F32)
+
+        def load_w(c, pieces):
+            is_key, idx = CHUNKS[c]
+            w = wk if is_key else wv
+            raw = rawp.tile([P, 4 * DIM], BF16, name="raw", tag="raw")
+            per = 4 // pieces
+            for i in range(pieces):
+                rows = w[idx * 512 + i * per * P: idx * 512 + (i + 1) * per * P, :]
+                nc.sync.dma_start(
+                    out=raw[:, i * per * DIM:(i + 1) * per * DIM].rearrange("p (t k) -> p t k", t=per),
+                    in_=rows.rearrange("(t p) k -> p t k", p=P),
+                )
+            raws[c] = raw[:].bitcast(F32)
+
+        ident = const.tile([P, P], F32, name="ident")
+        make_identity(nc, ident[:])
+        identb = const.tile([P, P], BF16, name="identb")
+        brows = const.tile([P, 512], BF16, name="brows")
+        cos_in = const.tile([P, HD], BF16, name="cos_in")
+        sin_in = const.tile([P, HD], BF16, name="sin_in")
+        cosf = const.tile([P, HD], F32, name="cosf")
+        sinf = const.tile([P, HD], F32, name="sinf")
+        bias_k = const.tile([P, H * HD], F32, name="bias_k")
+        bias_v = const.tile([P, H * HD], F32, name="bias_v")
+        xc = const.tile([P, 4 * 512], U32, name="xc", align_bytes=64)
+        xs = const.tile([P, 4 * 512], U8, name="xs", align_bytes=64)
+
+        nc.vector.memset(brows[:].bitcast(I32), 0)
+        nc.scalar.dma_start(out=brows[0:4, :], in_=bk.rearrange("(r c) -> r c", c=512))
+        nc.scalar.dma_start(out=brows[4:8, :], in_=bv.rearrange("(r c) -> r c", c=512))
+        nc.scalar.dma_start(out=cos_in[:], in_=cos.rearrange("a b s d -> (a b s) d"))
+        nc.scalar.dma_start(out=sin_in[:], in_=sin.rearrange("a b s d -> (a b s) d"))
+        load_x()
+        load_w(0, 4)
+        load_w(1, 2)
+        load_w(2, 2)
+        load_w(3, 2)
+        nc.vector.tensor_copy(out=identb[:], in_=ident[:])
+        nc.vector.tensor_copy(out=cosf[:], in_=cos_in[:])
+        nc.vector.tensor_scalar_mul(out=sinf[:, 0:64], in0=sin_in[:, 0:64], scalar1=-1.0)
+        nc.vector.tensor_copy(out=sinf[:, 64:128], in_=sin_in[:, 64:128])
+        cos_b = cosf[:].unsqueeze(1).to_broadcast([P, 4, HD])
+        sin_lo = sinf[:, 0:64].unsqueeze(1).to_broadcast([P, 4, 64])
+        sin_hi = sinf[:, 64:128].unsqueeze(1).to_broadcast([P, 4, 64])
+
+        def broadcast_bias(row, dst, on_scalar):
+            bank = accp.tile([P, 512], F32, name="acc", tag="acc")
+            nc.tensor.matmul(
+                out=bank[:], lhsT=identb[:, row:row + 1].to_broadcast([P, P]), rhs=brows[:],
+                start=True, stop=True,
+            )
+            if on_scalar:
+                nc.scalar.copy(out=dst, in_=bank[:])
+            else:
+                nc.vector.tensor_copy(out=dst, in_=bank[:])
+
+        def transpose_bank(words, cols):
+            bank = tps.tile([P, 512], F32, name="tbank", tag="tbank")
+            for j in range(4):
+                nc.tensor.transpose(
+                    out=bank[:, j * P:(j + 1) * P], in_=words[:, cols[j]:cols[j] + 2 * P - 1:2], identity=ident[:]
+                )
+            return bank
+
+        def rows_to_grouped(words, t):
+            banks = [transpose_bank(words, [t * 1024 + gp * 512 + 256 * (j // 2) + (j % 2) for j in range(4)]) for gp in range(2)]
+            grouped = grp.tile([P, 2048], BF16, name="grouped", tag="grouped", align_bytes=64)
+            gw = grouped[:].bitcast(F32)
+            for gp in range(2):
+                nc.scalar.copy(
+                    out=gw[:, gp * 512:(gp + 1) * 512].rearrange("p (g r u) -> p g r u", g=2, u=2),
+                    in_=banks[gp][:].rearrange("p (g u r) -> p g r u", g=2, u=2),
+                )
+            return grouped
+
+        def pass_to_grouped(words, g):
+            banks = [
+                transpose_bank(words, [(2 * fp + (j % 2)) * 1024 + 256 * g + (j // 2) for j in range(4)])
+                for fp in range(2)
+            ]
+            grouped = grp.tile([P, 2048], BF16, name="grouped", tag="grouped", align_bytes=64)
+            gw = grouped[:].bitcast(F32)
+            for fp in range(2):
+                nc.scalar.copy(
+                    out=gw[:, fp * 512:(fp + 1) * 512].rearrange("p (f u) -> p f u", u=2),
+                    in_=banks[fp][:].rearrange("p (u f) -> p f u", u=2),
+                )
+            return grouped
+
+        def quantise(grouped, codes, scales, part):
+            cols = slice(part * 512, (part + 1) * 512)
+            nc.vector.quantize_mx(out=codes[:, cols].bitcast(FP8X4), scales=scales[:, cols], in_=grouped[:])
+
+        wq = {}
+
+        def new_wq(c):
+            wc = wqp.tile([P, 4 * 512], U32, name="wc", tag="wc", align_bytes=64)
+            ws = wqp.tile([P, 4 * 512], U8, name="ws", tag="ws", align_bytes=64)
+            wq[c] = (wc, ws)
+
+        def mx(acc_cols, c, b, w_of_g, n):
+            wc, ws = wq[c]
+            for g in range(4):
+                xcols = slice(b * 512 + g * P, b * 512 + (g + 1) * P)
+                wcols = slice(w_of_g(g), w_of_g(g) + n)
+                nc.tensor.matmul_mx(
+                    out=acc_cols,
+                    lhsT=xc[:, xcols].bitcast(FP8X4), lhsT_scale=xs[:, xcols],
+                    rhs=wc[:, wcols].bitcast(FP8X4), rhs_scale=ws[:, wcols],
+                    start=(g == 0), stop=(g == 3),
+                )
+
+        def mx_group(c, b):
+            acc = accp.tile([P, 512], F32, name="acc", tag="acc")
+            mx(acc[:], c, b, lambda g: g * 512, 512)
+            return acc
+
+        deferred = []
+        cursor = [0]
+
+        def run_deferred(n):
+            for i in range(n):
+                if cursor[0] < len(deferred):
+                    deferred[cursor[0]]()
+                    cursor[0] = cursor[0] + 1
+
+        def store(dram, b, idx, o):
+            nc.sync.dma_start(
+                out=dram[b, idx * 4:(idx + 1) * 4, :, :].rearrange("h s d -> s h d"),
+                in_=o[:].rearrange("p (h d) -> p h d", h=4),
+            )
+
+        def evacuate(c, b, acc):
+            is_key, idx = CHUNKS[c]
+            cols = slice(idx * 512, (idx + 1) * 512)
+            if not is_key:
+                o = outp.tile([P, 512], F32, name="o", tag="o")
+                nc.vector.tensor_tensor(out=o[:], in0=acc[:], in1=bias_v[:, cols], op=ADD)
+                store(out_1, b, idx, o)
+                return
+            pb = tmpp.tile([P, 512], F32, name="pb", tag="pb")
+            nc.vector.tensor_tensor(out=pb[:], in0=acc[:], in1=bias_k[:, cols], op=ADD)
+            pbv = pb[:].rearrange("p (h d) -> p h d", h=4)
+            held = {}
+
+            def mul_sin():
+                t2 = tmpp.tile([P, 512], F32, name="t2", tag="t2")
+                t2v = t2[:].rearrange("p (h d) -> p h d", h=4)
+                eng = nc.gpsimd if SIN_ON_GPSIMD else nc.vector
+                eng.tensor_tensor(out=t2v[:, :, 0:64], in0=pbv[:, :, 64:128], in1=sin_lo, op=MULT)
+                eng.tensor_tensor(out=t2v[:, :, 64:128], in0=pbv[:, :, 0:64], in1=sin_hi, op=MULT)
+                held["t2"] = t2
+
+            def mul_cos():
+                o = outp.tile([P, 512], F32, name="o", tag="o")
+                nc.vector.tensor_tensor(
+                    out=o[:].rearrange("p (h d) -> p h d", h=4), in0=pbv, in1=cos_b, op=MULT
+                )
+                held["o"] = o
+
+            def combine():
+                o = held["o"]
+                nc.vector.tensor_tensor(out=o[:], in0=o[:], in1=held["t2"][:], op=ADD)
+                store(out_0, b, idx, o)
+
+            if SIN_ON_GPSIMD:
+                mul_sin()
+                deferred.extend([mul_cos, combine])
+            else:
+                deferred.extend([mul_cos, mul_sin, combine])
+
+        gx = {}
+        gx[0] = rows_to_grouped(raws["x"], 0)
+        gx[1] = rows_to_grouped(raws["x"], 1)
+        quantise(gx[0], xc, xs, 0)
+        for r in range(2):
+            broadcast_bias(r, bias_k[:, r * 512:(r + 1) * 512], False)
+        gx[2] = rows_to_grouped(raws["x"], 2)
+        quantise(gx[1], xc, xs, 1)
+        for r in range(2, 4):
+            broadcast_bias(r, bias_k[:, r * 512:(r + 1) * 512], False)
+        gx[3] = rows_to_grouped(raws["x"], 3)
+        quantise(gx[2], xc, xs, 2)
+        for r in range(2):
+            broadcast_bias(4 + r, bias_v[:, r * 512:(r + 1) * 512], False)
+
+        new_wq(0)
+        wc0, ws0 = wq[0]
+        gw0 = {}
+        acc0 = {}
+
+        def mx_first(f):
+            for b in range(B):
+                if f == 0:
+                    acc0[b] = accp.tile([P, 512], F32, name="acc", tag="acc")
+                mx(acc0[b][:, f * P:(f + 1) * P], 0, b, lambda g: f * 512 + g * P, P)
+
+        gw0[0] = rows_to_grouped(raws[0], 0)
+        quantise(gx[3], xc, xs, 3)
+        for r in range(2, 4):
+            broadcast_bias(4 + r, bias_v[:, r * 512:(r + 1) * 512], False)
+        gw0[1] = rows_to_grouped(raws[0], 1)
+        quantise(gw0[0], wc0, ws0, 0)
+        gw0[2] = rows_to_grouped(raws[0], 2)
+        quantise(gw0[1], wc0, ws0, 1)
+        mx_first(0)
+        gw0[3] = rows_to_grouped(raws[0], 3)
+        quantise(gw0[2], wc0, ws0, 2)
+        mx_first(1)
+        mx_first(2)
+        new_wq(1)
+        wc1, ws1 = wq[1]
+        g10 = pass_to_grouped(raws[1], 0)
+        g11 = pass_to_grouped(raws[1], 1)
+        quantise(gw0[3], wc0, ws0, 3)
+        mx_first(3)
+        quantise(g10, wc1, ws1, 0)
+        evacuate(0, 0, acc0[0])
+        quantise(g11, wc1, ws1, 1)
+        evacuate(0, 1, acc0[1])
+        g12 = pass_to_grouped(raws[1], 2)
+        g13 = pass_to_grouped(raws[1], 3)
+        evacuate(0, 2, acc0[2])
+        evacuate(0, 3, acc0[3])
+        load_w(4, 2)
+        run_deferred(1)
+        quantise(g12, wc1, ws1, 2)
+        run_deferred(1)
+        quantise(g13, wc1, ws1, 3)
+
+        for c in range(1, LAST + 1):
+            more = c < LAST
+            for half in range(2):
+                if more:
+                    if half == 0:
+                        new_wq(c + 1)
+                    wcn, wsn = wq[c + 1]
+                    ga = pass_to_grouped(raws[c + 1], 2 * half)
+                    gb = pass_to_grouped(raws[c + 1], 2 * half + 1)
+                run_deferred(DEFER_A)
+                if more:
+                    quantise(ga, wcn, wsn, 2 * half)
+                acc_a = mx_group(c, 2 * half)
+                acc_b = mx_group(c, 2 * half + 1)
+                run_deferred(DEFER_B)
+                evacuate(c, 2 * half, acc_a)
+                if more:
+                    quantise(gb, wcn, wsn, 2 * half + 1)
+                evacuate(c, 2 * half + 1, acc_b)
+            if c + 4 <= LAST:
+                load_w(c + 4, 2)
+        run_deferred(len(deferred))

@@ -27,8 +27,9 @@ def tile_attention_pb_kernel(tc, key_value, wk, bk, wv, bv, cos, sin, out_0, out
     nc = tc.nc
     with ExitStack() as ctx:
         const = ctx.enter_context(tc.tile_pool(name="const", bufs=1))
-        rawp = ctx.enter_context(tc.tile_pool(name="rawp", bufs=6))
+        rawp = ctx.enter_context(tc.tile_pool(name="rawp", bufs=5))
         grp = ctx.enter_context(tc.tile_pool(name="grp", bufs=6))
+        permp = ctx.enter_context(tc.tile_pool(name="permp", bufs=8))
         wqp = ctx.enter_context(tc.tile_pool(name="wqp", bufs=2))
         outp = ctx.enter_context(tc.tile_pool(name="outp", bufs=12))
         tmpp = ctx.enter_context(tc.tile_pool(name="tmpp", bufs=4))
@@ -99,16 +100,33 @@ def tile_attention_pb_kernel(tc, key_value, wk, bk, wv, bv, cos, sin, out_0, out
             else:
                 nc.vector.tensor_copy(out=dst, in_=bank[:])
 
-        def transpose_bank(words, cols):
+        def transpose_bank(sources):
             bank = tps.tile([P, 512], F32, name="tbank", tag="tbank")
             for j in range(4):
-                nc.tensor.transpose(
-                    out=bank[:, j * P:(j + 1) * P], in_=words[:, cols[j]:cols[j] + 2 * P - 1:2], identity=ident[:]
-                )
+                nc.tensor.transpose(out=bank[:, j * P:(j + 1) * P], in_=sources[j], identity=ident[:])
             return bank
 
-        def rows_to_grouped(words, t):
-            banks = [transpose_bank(words, [t * 1024 + gp * 512 + 256 * (j // 2) + (j % 2) for j in range(4)]) for gp in range(2)]
+        perms = {}
+
+        def permute(c, t):
+            if c > LAST:
+                return
+            perm = permp.tile([P, 1024], F32, name="perm", tag="perm")
+            nc.scalar.copy(
+                out=perm[:].rearrange("p (g u k) -> p g u k", g=4, u=2),
+                in_=raws[c][:, t * 1024:(t + 1) * 1024].rearrange("p (g k u) -> p g u k", g=4, u=2),
+            )
+            perms[(c, t)] = perm
+
+        def words_of(c, t, g, u):
+            if (c, t) in perms:
+                start = 256 * g + 128 * u
+                return perms[(c, t)][:, start:start + P]
+            start = t * 1024 + 256 * g + u
+            return raws[c][:, start:start + 2 * P - 1:2]
+
+        def rows_to_grouped(c, t):
+            banks = [transpose_bank([words_of(c, t, 2 * gp + j // 2, j % 2) for j in range(4)]) for gp in range(2)]
             grouped = grp.tile([P, 2048], BF16, name="grouped", tag="grouped", align_bytes=64)
             gw = grouped[:].bitcast(F32)
             for gp in range(2):
@@ -118,9 +136,9 @@ def tile_attention_pb_kernel(tc, key_value, wk, bk, wv, bv, cos, sin, out_0, out
                 )
             return grouped
 
-        def pass_to_grouped(words, g):
+        def pass_to_grouped(c, g):
             banks = [
-                transpose_bank(words, [(2 * fp + (j % 2)) * 1024 + 256 * g + (j // 2) for j in range(4)])
+                transpose_bank([words_of(c, 2 * fp + (j % 2), g, j // 2) for j in range(4)])
                 for fp in range(2)
             ]
             grouped = grp.tile([P, 2048], BF16, name="grouped", tag="grouped", align_bytes=64)
@@ -215,16 +233,16 @@ def tile_attention_pb_kernel(tc, key_value, wk, bk, wv, bv, cos, sin, out_0, out
                 deferred.extend([mul_cos, mul_sin, combine])
 
         gx = {}
-        gx[0] = rows_to_grouped(raws["x"], 0)
-        gx[1] = rows_to_grouped(raws["x"], 1)
+        gx[0] = rows_to_grouped("x", 0)
+        gx[1] = rows_to_grouped("x", 1)
         quantise(gx[0], xc, xs, 0)
         for r in range(2):
             broadcast_bias(r, bias_k[:, r * 512:(r + 1) * 512], False)
-        gx[2] = rows_to_grouped(raws["x"], 2)
+        gx[2] = rows_to_grouped("x", 2)
         quantise(gx[1], xc, xs, 1)
         for r in range(2, 4):
             broadcast_bias(r, bias_k[:, r * 512:(r + 1) * 512], False)
-        gx[3] = rows_to_grouped(raws["x"], 3)
+        gx[3] = rows_to_grouped("x", 3)
         quantise(gx[2], xc, xs, 2)
         for r in range(2):
             broadcast_bias(4 + r, bias_v[:, r * 512:(r + 1) * 512], False)
@@ -240,31 +258,34 @@ def tile_attention_pb_kernel(tc, key_value, wk, bk, wv, bv, cos, sin, out_0, out
                     acc0[b] = accp.tile([P, 512], F32, name="acc", tag="acc")
                 mx(acc0[b][:, f * P:(f + 1) * P], 0, b, lambda g: f * 512 + g * P, P)
 
-        gw0[0] = rows_to_grouped(raws[0], 0)
+        gw0[0] = rows_to_grouped(0, 0)
         quantise(gx[3], xc, xs, 3)
         for r in range(2, 4):
             broadcast_bias(4 + r, bias_v[:, r * 512:(r + 1) * 512], False)
-        gw0[1] = rows_to_grouped(raws[0], 1)
+        gw0[1] = rows_to_grouped(0, 1)
         quantise(gw0[0], wc0, ws0, 0)
-        gw0[2] = rows_to_grouped(raws[0], 2)
+        gw0[2] = rows_to_grouped(0, 2)
         quantise(gw0[1], wc0, ws0, 1)
         mx_first(0)
-        gw0[3] = rows_to_grouped(raws[0], 3)
+        gw0[3] = rows_to_grouped(0, 3)
         quantise(gw0[2], wc0, ws0, 2)
         mx_first(1)
         mx_first(2)
         new_wq(1)
         wc1, ws1 = wq[1]
-        g10 = pass_to_grouped(raws[1], 0)
-        g11 = pass_to_grouped(raws[1], 1)
+        g10 = pass_to_grouped(1, 0)
+        g11 = pass_to_grouped(1, 1)
         quantise(gw0[3], wc0, ws0, 3)
         mx_first(3)
         quantise(g10, wc1, ws1, 0)
         evacuate(0, 0, acc0[0])
         quantise(g11, wc1, ws1, 1)
         evacuate(0, 1, acc0[1])
-        g12 = pass_to_grouped(raws[1], 2)
-        g13 = pass_to_grouped(raws[1], 3)
+        g12 = pass_to_grouped(1, 2)
+        permute(2, 0)
+        g13 = pass_to_grouped(1, 3)
+        permute(2, 1)
+        permute(2, 2)
         evacuate(0, 2, acc0[2])
         evacuate(0, 3, acc0[3])
         load_w(4, 2)
@@ -280,8 +301,11 @@ def tile_attention_pb_kernel(tc, key_value, wk, bk, wv, bv, cos, sin, out_0, out
                     if half == 0:
                         new_wq(c + 1)
                     wcn, wsn = wq[c + 1]
-                    ga = pass_to_grouped(raws[c + 1], 2 * half)
-                    gb = pass_to_grouped(raws[c + 1], 2 * half + 1)
+                    ga = pass_to_grouped(c + 1, 2 * half)
+                    permute(c + 2, 2 * half)
+                    gb = pass_to_grouped(c + 1, 2 * half + 1)
+                    if half == 0:
+                        permute(c + 2, 1)
                 run_deferred(DEFER_A)
                 if more:
                     quantise(ga, wcn, wsn, 2 * half)

@@ -16,9 +16,9 @@ P = 128
 B, S, DIM, H, HD = 4, 128, 2048, 16, 128
 FLOPS = 2 * B * S * DIM * 2 * H * HD
 
-SIN_ON_GPSIMD = False
 DEFER_A = 2
 DEFER_B = 1
+PERMUTED = 3
 CHUNKS = [(True, 0), (False, 0), (True, 1), (False, 1), (True, 2), (False, 2), (True, 3), (False, 3)]
 LAST = len(CHUNKS) - 1
 
@@ -27,89 +27,104 @@ def tile_attention_pb_kernel(tc, key_value, wk, bk, wv, bv, cos, sin, out_0, out
     nc = tc.nc
     with ExitStack() as ctx:
         const = ctx.enter_context(tc.tile_pool(name="const", bufs=1))
-        rawp = ctx.enter_context(tc.tile_pool(name="rawp", bufs=5))
+        rawp = ctx.enter_context(tc.tile_pool(name="rawp", bufs=6))
+        permp = ctx.enter_context(tc.tile_pool(name="permp", bufs=6))
         grp = ctx.enter_context(tc.tile_pool(name="grp", bufs=6))
-        permp = ctx.enter_context(tc.tile_pool(name="permp", bufs=8))
         wqp = ctx.enter_context(tc.tile_pool(name="wqp", bufs=2))
-        outp = ctx.enter_context(tc.tile_pool(name="outp", bufs=12))
+        outp = ctx.enter_context(tc.tile_pool(name="outp", bufs=10))
         tmpp = ctx.enter_context(tc.tile_pool(name="tmpp", bufs=4))
+        biasp = ctx.enter_context(tc.tile_pool(name="biasp", bufs=3))
         tps = ctx.enter_context(tc.psum_pool(name="tps", bufs=4))
         accp = ctx.enter_context(tc.psum_pool(name="accp", bufs=4))
         ctx.enter_context(tc.manual_schedule())
 
-        raws = {}
-
-        def load_x():
-            raw = rawp.tile([P, 4 * DIM], BF16, name="raw", tag="raw")
-            for b in range(B):
-                nc.sync.dma_start(out=raw[:, b * DIM:(b + 1) * DIM], in_=key_value[b])
-            raws["x"] = raw[:].bitcast(F32)
-
-        def load_w(c, pieces):
-            is_key, idx = CHUNKS[c]
-            w = wk if is_key else wv
-            raw = rawp.tile([P, 4 * DIM], BF16, name="raw", tag="raw")
-            per = 4 // pieces
-            for i in range(pieces):
-                rows = w[idx * 512 + i * per * P: idx * 512 + (i + 1) * per * P, :]
-                nc.sync.dma_start(
-                    out=raw[:, i * per * DIM:(i + 1) * per * DIM].rearrange("p (t k) -> p t k", t=per),
-                    in_=rows.rearrange("(t p) k -> p t k", p=P),
-                )
-            raws[c] = raw[:].bitcast(F32)
-
         ident = const.tile([P, P], F32, name="ident")
-        make_identity(nc, ident[:])
         identb = const.tile([P, P], BF16, name="identb")
         brows = const.tile([P, 512], BF16, name="brows")
         cos_in = const.tile([P, HD], BF16, name="cos_in")
         sin_in = const.tile([P, HD], BF16, name="sin_in")
         cosf = const.tile([P, HD], F32, name="cosf")
         sinf = const.tile([P, HD], F32, name="sinf")
-        bias_k = const.tile([P, H * HD], F32, name="bias_k")
-        bias_v = const.tile([P, H * HD], F32, name="bias_v")
         xc = const.tile([P, 4 * 512], U32, name="xc", align_bytes=64)
         xs = const.tile([P, 4 * 512], U8, name="xs", align_bytes=64)
 
+        raws = {}
+        xraw = rawp.tile([P, 4 * DIM], BF16, name="raw", tag="raw")
+        raws["x"] = xraw[:].bitcast(F32)
+
+        def load_x(b):
+            nc.sync.dma_start(out=xraw[:, b * DIM:(b + 1) * DIM], in_=key_value[b])
+
+        def weight_rows(c):
+            is_key, idx = CHUNKS[c]
+            return (wk if is_key else wv)[idx * 512:(idx + 1) * 512, :]
+
+        def new_raw(c):
+            raw = rawp.tile([P, 4 * DIM], BF16, name="raw", tag="raw")
+            raws[c] = raw[:].bitcast(F32)
+            return raw
+
+        def load_by_rows(c):
+            raw = new_raw(c)
+            for t in range(4):
+                nc.sync.dma_start(out=raw[:, t * DIM:(t + 1) * DIM], in_=weight_rows(c)[t * P:(t + 1) * P, :])
+
+        def load_by_columns(c):
+            raw = new_raw(c)
+            for half in range(2):
+                cols = slice(half * (DIM // 2), (half + 1) * (DIM // 2))
+                nc.sync.dma_start(
+                    out=raw[:].rearrange("p (t k) -> p t k", t=4)[:, :, cols],
+                    in_=weight_rows(c)[:, cols].rearrange("(t p) k -> p t k", p=P),
+                )
+
         nc.vector.memset(brows[:].bitcast(I32), 0)
+        load_x(0)
+        load_by_rows(0)
         nc.scalar.dma_start(out=brows[0:4, :], in_=bk.rearrange("(r c) -> r c", c=512))
         nc.scalar.dma_start(out=brows[4:8, :], in_=bv.rearrange("(r c) -> r c", c=512))
         nc.scalar.dma_start(out=cos_in[:], in_=cos.rearrange("a b s d -> (a b s) d"))
         nc.scalar.dma_start(out=sin_in[:], in_=sin.rearrange("a b s d -> (a b s) d"))
-        load_x()
-        load_w(0, 4)
-        load_w(1, 2)
-        load_w(2, 2)
-        load_w(3, 2)
+        load_x(1)
+        load_x(2)
+        load_x(3)
+        load_by_columns(1)
+        load_by_columns(2)
+        load_by_columns(3)
+        load_by_columns(4)
+        make_identity(nc, ident[:])
         nc.vector.tensor_copy(out=identb[:], in_=ident[:])
-        nc.vector.tensor_copy(out=cosf[:], in_=cos_in[:])
-        nc.vector.tensor_scalar_mul(out=sinf[:, 0:64], in0=sin_in[:, 0:64], scalar1=-1.0)
-        nc.vector.tensor_copy(out=sinf[:, 64:128], in_=sin_in[:, 64:128])
         cos_b = cosf[:].unsqueeze(1).to_broadcast([P, 4, HD])
-        sin_lo = sinf[:, 0:64].unsqueeze(1).to_broadcast([P, 4, 64])
-        sin_hi = sinf[:, 64:128].unsqueeze(1).to_broadcast([P, 4, 64])
+        sin_b = sinf[:].unsqueeze(1).to_broadcast([P, 4, HD])
 
-        def broadcast_bias(row, dst, on_scalar):
+        def rope_tables():
+            nc.vector.tensor_copy(out=cosf[:], in_=cos_in[:])
+            nc.vector.tensor_scalar_mul(out=sinf[:, 0:64], in0=sin_in[:, 0:64], scalar1=-1.0)
+            nc.vector.tensor_copy(out=sinf[:, 64:128], in_=sin_in[:, 64:128])
+
+        biases = {}
+
+        def bias_table(c, on_scalar):
+            if c > LAST:
+                return
+            is_key, idx = CHUNKS[c]
+            row = idx if is_key else 4 + idx
             bank = accp.tile([P, 512], F32, name="acc", tag="acc")
             nc.tensor.matmul(
                 out=bank[:], lhsT=identb[:, row:row + 1].to_broadcast([P, P]), rhs=brows[:],
                 start=True, stop=True,
             )
+            table = biasp.tile([P, 512], F32, name="bias", tag="bias")
             if on_scalar:
-                nc.scalar.copy(out=dst, in_=bank[:])
+                nc.scalar.copy(out=table[:], in_=bank[:])
             else:
-                nc.vector.tensor_copy(out=dst, in_=bank[:])
-
-        def transpose_bank(sources):
-            bank = tps.tile([P, 512], F32, name="tbank", tag="tbank")
-            for j in range(4):
-                nc.tensor.transpose(out=bank[:, j * P:(j + 1) * P], in_=sources[j], identity=ident[:])
-            return bank
+                nc.vector.tensor_copy(out=table[:], in_=bank[:])
+            biases[c] = table
 
         perms = {}
 
         def permute(c, t):
-            if c > LAST:
+            if c > LAST or t >= PERMUTED:
                 return
             perm = permp.tile([P, 1024], F32, name="perm", tag="perm")
             nc.scalar.copy(
@@ -125,6 +140,12 @@ def tile_attention_pb_kernel(tc, key_value, wk, bk, wv, bv, cos, sin, out_0, out
             start = t * 1024 + 256 * g + u
             return raws[c][:, start:start + 2 * P - 1:2]
 
+        def transpose_bank(sources):
+            bank = tps.tile([P, 512], F32, name="tbank", tag="tbank")
+            for j in range(4):
+                nc.tensor.transpose(out=bank[:, j * P:(j + 1) * P], in_=sources[j], identity=ident[:])
+            return bank
+
         def rows_to_grouped(c, t):
             banks = [transpose_bank([words_of(c, t, 2 * gp + j // 2, j % 2) for j in range(4)]) for gp in range(2)]
             grouped = grp.tile([P, 2048], BF16, name="grouped", tag="grouped", align_bytes=64)
@@ -137,10 +158,7 @@ def tile_attention_pb_kernel(tc, key_value, wk, bk, wv, bv, cos, sin, out_0, out
             return grouped
 
         def pass_to_grouped(c, g):
-            banks = [
-                transpose_bank([words_of(c, 2 * fp + (j % 2), g, j // 2) for j in range(4)])
-                for fp in range(2)
-            ]
+            banks = [transpose_bank([words_of(c, 2 * fp + (j % 2), g, j // 2) for j in range(4)]) for fp in range(2)]
             grouped = grp.tile([P, 2048], BF16, name="grouped", tag="grouped", align_bytes=64)
             gw = grouped[:].bitcast(F32)
             for fp in range(2):
@@ -150,10 +168,6 @@ def tile_attention_pb_kernel(tc, key_value, wk, bk, wv, bv, cos, sin, out_0, out
                 )
             return grouped
 
-        def quantise(grouped, codes, scales, part):
-            cols = slice(part * 512, (part + 1) * 512)
-            nc.vector.quantize_mx(out=codes[:, cols].bitcast(FP8X4), scales=scales[:, cols], in_=grouped[:])
-
         wq = {}
 
         def new_wq(c):
@@ -161,21 +175,35 @@ def tile_attention_pb_kernel(tc, key_value, wk, bk, wv, bv, cos, sin, out_0, out
             ws = wqp.tile([P, 4 * 512], U8, name="ws", tag="ws", align_bytes=64)
             wq[c] = (wc, ws)
 
-        def mx(acc_cols, c, b, w_of_g, n):
+        def quantise_x(grouped, b):
+            cols = slice(b * 512, (b + 1) * 512)
+            nc.vector.quantize_mx(out=xc[:, cols].bitcast(FP8X4), scales=xs[:, cols], in_=grouped[:])
+
+        def quantise_pass(grouped, c, g):
+            wc, ws = wq[c]
+            cols = slice(g * 512, (g + 1) * 512)
+            nc.vector.quantize_mx(out=wc[:, cols].bitcast(FP8X4), scales=ws[:, cols], in_=grouped[:])
+
+        def quantise_rows(grouped, c, t):
             wc, ws = wq[c]
             for g in range(4):
-                xcols = slice(b * 512 + g * P, b * 512 + (g + 1) * P)
-                wcols = slice(w_of_g(g), w_of_g(g) + n)
-                nc.tensor.matmul_mx(
-                    out=acc_cols,
-                    lhsT=xc[:, xcols].bitcast(FP8X4), lhsT_scale=xs[:, xcols],
-                    rhs=wc[:, wcols].bitcast(FP8X4), rhs_scale=ws[:, wcols],
-                    start=(g == 0), stop=(g == 3),
+                cols = slice(g * 512 + t * P, g * 512 + (t + 1) * P)
+                nc.vector.quantize_mx(
+                    out=wc[:, cols].bitcast(FP8X4), scales=ws[:, cols], in_=grouped[:, g * 512:(g + 1) * 512]
                 )
 
         def mx_group(c, b):
             acc = accp.tile([P, 512], F32, name="acc", tag="acc")
-            mx(acc[:], c, b, lambda g: g * 512, 512)
+            wc, ws = wq[c]
+            for g in range(4):
+                xcols = slice(b * 512 + g * P, b * 512 + (g + 1) * P)
+                wcols = slice(g * 512, (g + 1) * 512)
+                nc.tensor.matmul_mx(
+                    out=acc[:],
+                    lhsT=xc[:, xcols].bitcast(FP8X4), lhsT_scale=xs[:, xcols],
+                    rhs=wc[:, wcols].bitcast(FP8X4), rhs_scale=ws[:, wcols],
+                    start=(g == 0), stop=(g == 3),
+                )
             return acc
 
         deferred = []
@@ -195,29 +223,30 @@ def tile_attention_pb_kernel(tc, key_value, wk, bk, wv, bv, cos, sin, out_0, out
 
         def evacuate(c, b, acc):
             is_key, idx = CHUNKS[c]
-            cols = slice(idx * 512, (idx + 1) * 512)
+            bias = biases[c]
             if not is_key:
                 o = outp.tile([P, 512], F32, name="o", tag="o")
-                nc.vector.tensor_tensor(out=o[:], in0=acc[:], in1=bias_v[:, cols], op=ADD)
+                nc.vector.tensor_tensor(out=o[:], in0=acc[:], in1=bias[:], op=ADD)
                 store(out_1, b, idx, o)
                 return
             pb = tmpp.tile([P, 512], F32, name="pb", tag="pb")
-            nc.vector.tensor_tensor(out=pb[:], in0=acc[:], in1=bias_k[:, cols], op=ADD)
-            pbv = pb[:].rearrange("p (h d) -> p h d", h=4)
+            nc.vector.tensor_tensor(out=pb[:], in0=acc[:], in1=bias[:], op=ADD)
             held = {}
 
             def mul_sin():
                 t2 = tmpp.tile([P, 512], F32, name="t2", tag="t2")
-                t2v = t2[:].rearrange("p (h d) -> p h d", h=4)
-                eng = nc.gpsimd if SIN_ON_GPSIMD else nc.vector
-                eng.tensor_tensor(out=t2v[:, :, 0:64], in0=pbv[:, :, 64:128], in1=sin_lo, op=MULT)
-                eng.tensor_tensor(out=t2v[:, :, 64:128], in0=pbv[:, :, 0:64], in1=sin_hi, op=MULT)
+                nc.vector.tensor_tensor(
+                    out=t2[:].rearrange("p (h a i) -> p h a i", h=4, a=2),
+                    in0=pb[:].rearrange("p (h a i) -> p h a i", h=4, a=2)[:, :, ::-1, :],
+                    in1=sin_b.rearrange("p h (a i) -> p h a i", a=2), op=MULT,
+                )
                 held["t2"] = t2
 
             def mul_cos():
                 o = outp.tile([P, 512], F32, name="o", tag="o")
                 nc.vector.tensor_tensor(
-                    out=o[:].rearrange("p (h d) -> p h d", h=4), in0=pbv, in1=cos_b, op=MULT
+                    out=o[:].rearrange("p (h d) -> p h d", h=4), in0=pb[:].rearrange("p (h d) -> p h d", h=4),
+                    in1=cos_b, op=MULT,
                 )
                 held["o"] = o
 
@@ -226,73 +255,54 @@ def tile_attention_pb_kernel(tc, key_value, wk, bk, wv, bv, cos, sin, out_0, out
                 nc.vector.tensor_tensor(out=o[:], in0=o[:], in1=held["t2"][:], op=ADD)
                 store(out_0, b, idx, o)
 
-            if SIN_ON_GPSIMD:
-                mul_sin()
-                deferred.extend([mul_cos, combine])
-            else:
-                deferred.extend([mul_cos, mul_sin, combine])
-
-        gx = {}
-        gx[0] = rows_to_grouped("x", 0)
-        gx[1] = rows_to_grouped("x", 1)
-        quantise(gx[0], xc, xs, 0)
-        for r in range(2):
-            broadcast_bias(r, bias_k[:, r * 512:(r + 1) * 512], False)
-        gx[2] = rows_to_grouped("x", 2)
-        quantise(gx[1], xc, xs, 1)
-        for r in range(2, 4):
-            broadcast_bias(r, bias_k[:, r * 512:(r + 1) * 512], False)
-        gx[3] = rows_to_grouped("x", 3)
-        quantise(gx[2], xc, xs, 2)
-        for r in range(2):
-            broadcast_bias(4 + r, bias_v[:, r * 512:(r + 1) * 512], False)
+            deferred.extend([mul_cos, mul_sin, combine])
 
         new_wq(0)
-        wc0, ws0 = wq[0]
-        gw0 = {}
-        acc0 = {}
-
-        def mx_first(f):
-            for b in range(B):
-                if f == 0:
-                    acc0[b] = accp.tile([P, 512], F32, name="acc", tag="acc")
-                mx(acc0[b][:, f * P:(f + 1) * P], 0, b, lambda g: f * 512 + g * P, P)
-
-        gw0[0] = rows_to_grouped(0, 0)
-        quantise(gx[3], xc, xs, 3)
-        for r in range(2, 4):
-            broadcast_bias(4 + r, bias_v[:, r * 512:(r + 1) * 512], False)
-        gw0[1] = rows_to_grouped(0, 1)
-        quantise(gw0[0], wc0, ws0, 0)
-        gw0[2] = rows_to_grouped(0, 2)
-        quantise(gw0[1], wc0, ws0, 1)
-        mx_first(0)
-        gw0[3] = rows_to_grouped(0, 3)
-        quantise(gw0[2], wc0, ws0, 2)
-        mx_first(1)
-        mx_first(2)
+        gx = {}
+        gw = {}
+        gx[0] = rows_to_grouped("x", 0)
+        gw[0] = rows_to_grouped(0, 0)
+        quantise_x(gx[0], 0)
+        gw[1] = rows_to_grouped(0, 1)
+        quantise_rows(gw[0], 0, 0)
+        gw[2] = rows_to_grouped(0, 2)
+        quantise_rows(gw[1], 0, 1)
+        bias_table(0, False)
+        gw[3] = rows_to_grouped(0, 3)
+        quantise_rows(gw[2], 0, 2)
+        rope_tables()
+        gx[1] = rows_to_grouped("x", 1)
+        quantise_rows(gw[3], 0, 3)
+        gx[2] = rows_to_grouped("x", 2)
+        quantise_x(gx[1], 1)
+        acc = mx_group(0, 0)
+        gx[3] = rows_to_grouped("x", 3)
+        evacuate(0, 0, acc)
+        quantise_x(gx[2], 2)
+        acc = mx_group(0, 1)
+        bias_table(1, True)
+        run_deferred(1)
+        evacuate(0, 1, acc)
+        quantise_x(gx[3], 3)
+        acc = mx_group(0, 2)
         new_wq(1)
-        wc1, ws1 = wq[1]
-        g10 = pass_to_grouped(1, 0)
-        g11 = pass_to_grouped(1, 1)
-        quantise(gw0[3], wc0, ws0, 3)
-        mx_first(3)
-        quantise(g10, wc1, ws1, 0)
-        evacuate(0, 0, acc0[0])
-        quantise(g11, wc1, ws1, 1)
-        evacuate(0, 1, acc0[1])
-        g12 = pass_to_grouped(1, 2)
-        permute(2, 0)
-        g13 = pass_to_grouped(1, 3)
-        permute(2, 1)
-        permute(2, 2)
-        evacuate(0, 2, acc0[2])
-        evacuate(0, 3, acc0[3])
-        load_w(4, 2)
+        g0 = pass_to_grouped(1, 0)
+        run_deferred(2)
+        evacuate(0, 2, acc)
+        quantise_pass(g0, 1, 0)
+        acc = mx_group(0, 3)
+        g1 = pass_to_grouped(1, 1)
         run_deferred(1)
-        quantise(g12, wc1, ws1, 2)
+        evacuate(0, 3, acc)
+        quantise_pass(g1, 1, 1)
+        g2 = pass_to_grouped(1, 2)
+        g3 = pass_to_grouped(1, 3)
+        for t in range(4):
+            permute(2, t)
+        run_deferred(2)
+        quantise_pass(g2, 1, 2)
         run_deferred(1)
-        quantise(g13, wc1, ws1, 3)
+        quantise_pass(g3, 1, 3)
 
         for c in range(1, LAST + 1):
             more = c < LAST
@@ -300,22 +310,21 @@ def tile_attention_pb_kernel(tc, key_value, wk, bk, wv, bv, cos, sin, out_0, out
                 if more:
                     if half == 0:
                         new_wq(c + 1)
-                    wcn, wsn = wq[c + 1]
                     ga = pass_to_grouped(c + 1, 2 * half)
                     permute(c + 2, 2 * half)
                     gb = pass_to_grouped(c + 1, 2 * half + 1)
-                    if half == 0:
-                        permute(c + 2, 1)
+                    permute(c + 2, 2 * half + 1)
                 run_deferred(DEFER_A)
                 if more:
-                    quantise(ga, wcn, wsn, 2 * half)
+                    quantise_pass(ga, c + 1, 2 * half)
                 acc_a = mx_group(c, 2 * half)
                 acc_b = mx_group(c, 2 * half + 1)
                 run_deferred(DEFER_B)
                 evacuate(c, 2 * half, acc_a)
                 if more:
-                    quantise(gb, wcn, wsn, 2 * half + 1)
+                    quantise_pass(gb, c + 1, 2 * half + 1)
                 evacuate(c, 2 * half + 1, acc_b)
+            bias_table(c + 1, True)
             if c + 4 <= LAST:
-                load_w(c + 4, 2)
+                load_by_columns(c + 4)
         run_deferred(len(deferred))

@@ -69,6 +69,14 @@ def tile_attention_pb_kernel(tc, key_value, wk, bk, wv, bv, cos, sin, out_0, out
             for t in range(4):
                 nc.sync.dma_start(out=raw[:, t * DIM:(t + 1) * DIM], in_=weight_rows(c)[t * P:(t + 1) * P, :])
 
+        def load_by_row_pairs(c):
+            raw = new_raw(c)
+            for half in range(2):
+                nc.sync.dma_start(
+                    out=raw[:, half * 2 * DIM:(half + 1) * 2 * DIM].rearrange("p (t k) -> p t k", t=2),
+                    in_=weight_rows(c)[half * 2 * P:(half + 1) * 2 * P, :].rearrange("(t p) k -> p t k", p=P),
+                )
+
         def load_by_columns(c):
             raw = new_raw(c)
             for half in range(2):
@@ -78,6 +86,8 @@ def tile_attention_pb_kernel(tc, key_value, wk, bk, wv, bv, cos, sin, out_0, out
                     in_=weight_rows(c)[:, cols].rearrange("(t p) k -> p t k", p=P),
                 )
 
+        zeros = const.tile([P, 512], BF16, name="zeros")
+        nc.vector.memset(zeros[:].bitcast(I32), 0)
         nc.vector.memset(brows[:].bitcast(I32), 0)
         load_x(0)
         load_by_rows(0)
@@ -89,9 +99,9 @@ def tile_attention_pb_kernel(tc, key_value, wk, bk, wv, bv, cos, sin, out_0, out
         load_x(2)
         load_x(3)
         load_by_columns(1)
-        load_by_columns(2)
-        load_by_columns(3)
-        load_by_columns(4)
+        load_by_row_pairs(2)
+        load_by_row_pairs(3)
+        load_by_row_pairs(4)
         make_identity(nc, ident[:])
         nc.vector.tensor_copy(out=identb[:], in_=ident[:])
         cos_b = cosf[:].unsqueeze(1).to_broadcast([P, 4, HD])
@@ -257,22 +267,34 @@ def tile_attention_pb_kernel(tc, key_value, wk, bk, wv, bv, cos, sin, out_0, out
 
             deferred.extend([mul_cos, mul_sin, combine])
 
+        warm_bank = accp.tile([P, 512], F32, name="acc", tag="acc")
+
+        def keep_warm(n):
+            for i in range(n):
+                nc.tensor.matmul(out=warm_bank[:], lhsT=zeros[:, 0:P], rhs=zeros[:], start=True, stop=True)
+
         new_wq(0)
         gx = {}
         gw = {}
+        keep_warm(5)
         gx[0] = rows_to_grouped("x", 0)
+        keep_warm(1)
         gw[0] = rows_to_grouped(0, 0)
         quantise_x(gx[0], 0)
+        keep_warm(1)
         gw[1] = rows_to_grouped(0, 1)
         quantise_rows(gw[0], 0, 0)
+        bias_table(0, False)
         gw[2] = rows_to_grouped(0, 2)
         quantise_rows(gw[1], 0, 1)
-        bias_table(0, False)
+        bias_table(1, False)
         gw[3] = rows_to_grouped(0, 3)
         quantise_rows(gw[2], 0, 2)
         rope_tables()
+        keep_warm(1)
         gx[1] = rows_to_grouped("x", 1)
         quantise_rows(gw[3], 0, 3)
+        keep_warm(1)
         gx[2] = rows_to_grouped("x", 2)
         quantise_x(gx[1], 1)
         acc = mx_group(0, 0)
@@ -280,7 +302,6 @@ def tile_attention_pb_kernel(tc, key_value, wk, bk, wv, bv, cos, sin, out_0, out
         evacuate(0, 0, acc)
         quantise_x(gx[2], 2)
         acc = mx_group(0, 1)
-        bias_table(1, True)
         run_deferred(1)
         evacuate(0, 1, acc)
         quantise_x(gx[3], 3)
@@ -326,5 +347,5 @@ def tile_attention_pb_kernel(tc, key_value, wk, bk, wv, bv, cos, sin, out_0, out
                 evacuate(c, 2 * half + 1, acc_b)
             bias_table(c + 1, True)
             if c + 4 <= LAST:
-                load_by_columns(c + 4)
+                load_by_row_pairs(c + 4)
         run_deferred(len(deferred))

@@ -333,13 +333,14 @@ def tile_attention_pb_kernel(tc, key_value, wk, bk, wv, bv, cos, sin, out_0, out
                         new_wq(c + 1)
                     ga = pass_to_grouped(c + 1, 2 * half)
                     permute(c + 2, 2 * half)
+                acc_a = mx_group(c, 2 * half)
+                if more:
                     gb = pass_to_grouped(c + 1, 2 * half + 1)
                     permute(c + 2, 2 * half + 1)
+                acc_b = mx_group(c, 2 * half + 1)
                 run_deferred(DEFER_A)
                 if more:
                     quantise_pass(ga, c + 1, 2 * half)
-                acc_a = mx_group(c, 2 * half)
-                acc_b = mx_group(c, 2 * half + 1)
                 run_deferred(DEFER_B)
                 evacuate(c, 2 * half, acc_a)
                 if more:

@@ -18,7 +18,7 @@ FLOPS = 2 * B * S * DIM * 2 * H * HD
 
 DEFER_A = 2
 DEFER_B = 1
-PERMUTED = 3
+PERMUTED = 0
 CHUNKS = [(True, 0), (False, 0), (True, 1), (False, 1), (True, 2), (False, 2), (True, 3), (False, 3)]
 LAST = len(CHUNKS) - 1
 

@@ -18,7 +18,7 @@ FLOPS = 2 * B * S * DIM * 2 * H * HD
 
 DEFER_A = 2
 DEFER_B = 1
-PERMUTED = 0
+PERMUTED = 2
 CHUNKS = [(True, 0), (False, 0), (True, 1), (False, 1), (True, 2), (False, 2), (True, 3), (False, 3)]
 LAST = len(CHUNKS) - 1
 
@@ -133,15 +133,16 @@ def tile_attention_pb_kernel(tc, key_value, wk, bk, wv, bv, cos, sin, out_0, out
 
         perms = {}
 
-        def permute(c, t):
+        def permute(c, piece):
+            t, half = divmod(piece, 2)
             if c > LAST or t >= PERMUTED:
                 return
-            perm = permp.tile([P, 1024], F32, name="perm", tag="perm")
+            if half == 0:
+                perms[(c, t)] = permp.tile([P, 1024], F32, name="perm", tag="perm")
             nc.scalar.copy(
-                out=perm[:].rearrange("p (g u k) -> p g u k", g=4, u=2),
-                in_=raws[c][:, t * 1024:(t + 1) * 1024].rearrange("p (g k u) -> p g u k", g=4, u=2),
+                out=perms[(c, t)][:, half * 512:(half + 1) * 512].rearrange("p (g u k) -> p g u k", g=2, u=2),
+                in_=raws[c][:, t * 1024 + half * 512:t * 1024 + (half + 1) * 512].rearrange("p (g k u) -> p g u k", g=2, u=2),
             )
-            perms[(c, t)] = perm
 
         def words_of(c, t, g, u):
             if (c, t) in perms:
@@ -318,8 +319,6 @@ def tile_attention_pb_kernel(tc, key_value, wk, bk, wv, bv, cos, sin, out_0, out
         quantise_pass(g1, 1, 1)
         g2 = pass_to_grouped(1, 2)
         g3 = pass_to_grouped(1, 3)
-        for t in range(4):
-            permute(2, t)
         run_deferred(2)
         quantise_pass(g2, 1, 2)
         run_deferred(1)
@@ -327,6 +326,8 @@ def tile_attention_pb_kernel(tc, key_value, wk, bk, wv, bv, cos, sin, out_0, out
 
         for c in range(1, LAST + 1):
             more = c < LAST
+            if c + 4 <= LAST:
+                load_by_row_pairs(c + 4)
             for half in range(2):
                 if more:
                     if half == 0:
@@ -347,6 +348,4 @@ def tile_attention_pb_kernel(tc, key_value, wk, bk, wv, bv, cos, sin, out_0, out
                     quantise_pass(gb, c + 1, 2 * half + 1)
                 evacuate(c, 2 * half + 1, acc_b)
             bias_table(c + 1, True)
-            if c + 4 <= LAST:
-                load_by_row_pairs(c + 4)
         run_deferred(len(deferred))

@@ -73,18 +73,19 @@ def tile_attention_pb_kernel(tc, key_value, wk, bk, wv, bv, cos, sin, out_0, out
             raw = new_raw(c)
             for half in range(2):
                 nc.sync.dma_start(
-                    out=raw[:, half * 2 * DIM:(half + 1) * 2 * DIM].rearrange("p (t k) -> p t k", t=2),
-                    in_=weight_rows(c)[half * 2 * P:(half + 1) * 2 * P, :].rearrange("(t p) k -> p t k", p=P),
+                    out=raw[:, half * 2 * DIM:(half + 1) * 2 * DIM],
+                    in_=weight_rows(c)[half * 2 * P:(half + 1) * 2 * P, :].rearrange("(p t) k -> p (t k)", t=2),
                 )
 
         def load_by_columns(c):
             raw = new_raw(c)
             for half in range(2):
                 cols = slice(half * (DIM // 2), (half + 1) * (DIM // 2))
-                nc.sync.dma_start(
-                    out=raw[:].rearrange("p (t k) -> p t k", t=4)[:, :, cols],
-                    in_=weight_rows(c)[:, cols].rearrange("(t p) k -> p t k", p=P),
-                )
+                for pair in range(2):
+                    nc.sync.dma_start(
+                        out=raw[:].rearrange("p (t k) -> p t k", t=4)[:, 2 * pair:2 * pair + 2, cols],
+                        in_=weight_rows(c)[pair * 2 * P:(pair + 1) * 2 * P, cols].rearrange("(p t) k -> p t k", t=2),
+                    )
 
         zeros = const.tile([P, 512], BF16, name="zeros")
         nc.vector.memset(zeros[:].bitcast(I32), 0)
@@ -139,10 +140,12 @@ def tile_attention_pb_kernel(tc, key_value, wk, bk, wv, bv, cos, sin, out_0, out
                 return
             if half == 0:
                 perms[(c, t)] = permp.tile([P, 1024], F32, name="perm", tag="perm")
-            nc.scalar.copy(
-                out=perms[(c, t)][:, half * 512:(half + 1) * 512].rearrange("p (g u k) -> p g u k", g=2, u=2),
-                in_=raws[c][:, t * 1024 + half * 512:t * 1024 + (half + 1) * 512].rearrange("p (g k u) -> p g u k", g=2, u=2),
-            )
+            for g in (2 * half, 2 * half + 1):
+                src = raws[c][:, t * 1024 + 256 * g:t * 1024 + 256 * (g + 1)]
+                nc.scalar.copy(
+                    out=perms[(c, t)][:, 256 * g:256 * (g + 1)].rearrange("p (u k i) -> p k u i", u=2, i=4),
+                    in_=src.rearrange("p (k i u) -> p k u i", i=4, u=2),
+                )
 
         def words_of(c, t, g, u):
             if (c, t) in perms:
@@ -174,8 +177,8 @@ def tile_attention_pb_kernel(tc, key_value, wk, bk, wv, bv, cos, sin, out_0, out
             gw = grouped[:].bitcast(F32)
             for fp in range(2):
                 nc.scalar.copy(
-                    out=gw[:, fp * 512:(fp + 1) * 512].rearrange("p (f u) -> p f u", u=2),
-                    in_=banks[fp][:].rearrange("p (u f) -> p f u", u=2),
+                    out=gw[:, fp * 512:(fp + 1) * 512].rearrange("p (r t u) -> p r t u", t=2, u=2),
+                    in_=banks[fp][:].rearrange("p (u t r) -> p r t u", t=2, u=2),
                 )
             return grouped
 
@@ -263,8 +266,16 @@ def tile_attention_pb_kernel(tc, key_value, wk, bk, wv, bv, cos, sin, out_0, out
 
             def combine():
                 o = held["o"]
-                nc.vector.tensor_tensor(out=o[:], in0=o[:], in1=held["t2"][:], op=ADD)
-                store(out_0, b, idx, o)
+                last_key = (idx, b) == (3, B - 1)
+                pieces = 2 if last_key else 1
+                heads = 4 // pieces
+                for i in range(pieces):
+                    part = slice(i * heads * HD, (i + 1) * heads * HD)
+                    nc.vector.tensor_tensor(out=o[:, part], in0=o[:, part], in1=held["t2"][:, part], op=ADD)
+                    nc.sync.dma_start(
+                        out=out_0[b, idx * 4 + i * heads:idx * 4 + (i + 1) * heads, :, :].rearrange("h s d -> s h d"),
+                        in_=o[:, part].rearrange("p (h d) -> p h d", d=HD),
+                    )
 
             deferred.extend([mul_cos, mul_sin, combine])
 

from contextlib import ExitStack

import concourse.mybir as mybir
from concourse.masks import make_identity

F32 = mybir.dt.float32
BF16 = mybir.dt.bfloat16
U32 = mybir.dt.uint32
U8 = mybir.dt.uint8
I32 = mybir.dt.int32
FP8X4 = mybir.dt.float8_e4m3fn_x4
ADD = mybir.AluOpType.add
MULT = mybir.AluOpType.mult

P = 128
B, S, DIM, H, HD = 4, 128, 2048, 16, 128
FLOPS = 2 * B * S * DIM * 2 * H * HD

DEFER_A = 2
DEFER_B = 1
PERMUTED = 2
CHUNKS = [(True, 0), (False, 0), (True, 1), (False, 1), (True, 2), (False, 2), (True, 3), (False, 3)]
LAST = len(CHUNKS) - 1


def tile_attention_pb_kernel(tc, key_value, wk, bk, wv, bv, cos, sin, out_0, out_1):
    nc = tc.nc
    with ExitStack() as ctx:
        const = ctx.enter_context(tc.tile_pool(name="const", bufs=1))
        rawp = ctx.enter_context(tc.tile_pool(name="rawp", bufs=6))
        permp = ctx.enter_context(tc.tile_pool(name="permp", bufs=6))
        grp = ctx.enter_context(tc.tile_pool(name="grp", bufs=6))
        wqp = ctx.enter_context(tc.tile_pool(name="wqp", bufs=2))
        outp = ctx.enter_context(tc.tile_pool(name="outp", bufs=10))
        tmpp = ctx.enter_context(tc.tile_pool(name="tmpp", bufs=4))
        biasp = ctx.enter_context(tc.tile_pool(name="biasp", bufs=3))
        tps = ctx.enter_context(tc.psum_pool(name="tps", bufs=4))
        accp = ctx.enter_context(tc.psum_pool(name="accp", bufs=4))
        ctx.enter_context(tc.manual_schedule())

        ident = const.tile([P, P], F32, name="ident")
        identb = const.tile([P, P], BF16, name="identb")
        brows = const.tile([P, 512], BF16, name="brows")
        cos_in = const.tile([P, HD], BF16, name="cos_in")
        sin_in = const.tile([P, HD], BF16, name="sin_in")
        cosf = const.tile([P, HD], F32, name="cosf")
        sinf = const.tile([P, HD], F32, name="sinf")
        xc = const.tile([P, 4 * 512], U32, name="xc", align_bytes=64)
        xs = const.tile([P, 4 * 512], U8, name="xs", align_bytes=64)

        raws = {}
        xraw = rawp.tile([P, 4 * DIM], BF16, name="raw", tag="raw")
        raws["x"] = xraw[:].bitcast(F32)

        def load_x(b):
            nc.sync.dma_start(out=xraw[:, b * DIM:(b + 1) * DIM], in_=key_value[b])

        def weight_rows(c):
            is_key, idx = CHUNKS[c]
            return (wk if is_key else wv)[idx * 512:(idx + 1) * 512, :]

        def new_raw(c):
            raw = rawp.tile([P, 4 * DIM], BF16, name="raw", tag="raw")
            raws[c] = raw[:].bitcast(F32)
            return raw

        def load_by_rows(c):
            raw = new_raw(c)
            for t in range(4):
                nc.sync.dma_start(out=raw[:, t * DIM:(t + 1) * DIM], in_=weight_rows(c)[t * P:(t + 1) * P, :])

        def load_by_row_pairs(c):
            raw = new_raw(c)
            for half in range(2):
                nc.sync.dma_start(
                    out=raw[:, half * 2 * DIM:(half + 1) * 2 * DIM],
                    in_=weight_rows(c)[half * 2 * P:(half + 1) * 2 * P, :].rearrange("(p t) k -> p (t k)", t=2),
                )

        def load_by_columns(c):
            raw = new_raw(c)
            for half in range(2):
                cols = slice(half * (DIM // 2), (half + 1) * (DIM // 2))
                for pair in range(2):
                    nc.sync.dma_start(
                        out=raw[:].rearrange("p (t k) -> p t k", t=4)[:, 2 * pair:2 * pair + 2, cols],
                        in_=weight_rows(c)[pair * 2 * P:(pair + 1) * 2 * P, cols].rearrange("(p t) k -> p t k", t=2),
                    )

        zeros = const.tile([P, 512], BF16, name="zeros")
        nc.vector.memset(zeros[:].bitcast(I32), 0)
        nc.vector.memset(brows[:].bitcast(I32), 0)
        load_x(0)
        load_by_rows(0)
        nc.scalar.dma_start(out=brows[0:4, :], in_=bk.rearrange("(r c) -> r c", c=512))
        nc.scalar.dma_start(out=brows[4:8, :], in_=bv.rearrange("(r c) -> r c", c=512))
        nc.scalar.dma_start(out=cos_in[:], in_=cos.rearrange("a b s d -> (a b s) d"))
        nc.scalar.dma_start(out=sin_in[:], in_=sin.rearrange("a b s d -> (a b s) d"))
        load_x(1)
        load_x(2)
        load_x(3)
        load_by_columns(1)
        load_by_row_pairs(2)
        load_by_row_pairs(3)
        load_by_row_pairs(4)
        make_identity(nc, ident[:])
        nc.vector.tensor_copy(out=identb[:], in_=ident[:])
        cos_b = cosf[:].unsqueeze(1).to_broadcast([P, 4, HD])
        sin_b = sinf[:].unsqueeze(1).to_broadcast([P, 4, HD])

        def rope_tables():
            nc.vector.tensor_copy(out=cosf[:], in_=cos_in[:])
            nc.vector.tensor_scalar_mul(out=sinf[:, 0:64], in0=sin_in[:, 0:64], scalar1=-1.0)
            nc.vector.tensor_copy(out=sinf[:, 64:128], in_=sin_in[:, 64:128])

        biases = {}

        def bias_table(c, on_scalar):
            if c > LAST:
                return
            is_key, idx = CHUNKS[c]
            row = idx if is_key else 4 + idx
            bank = accp.tile([P, 512], F32, name="acc", tag="acc")
            nc.tensor.matmul(
                out=bank[:], lhsT=identb[:, row:row + 1].to_broadcast([P, P]), rhs=brows[:],
                start=True, stop=True,
            )
            table = biasp.tile([P, 512], F32, name="bias", tag="bias")
            if on_scalar:
                nc.scalar.copy(out=table[:], in_=bank[:])
            else:
                nc.vector.tensor_copy(out=table[:], in_=bank[:])
            biases[c] = table

        perms = {}

        def permute(c, piece):
            t, half = divmod(piece, 2)
            if c > LAST or t >= PERMUTED:
                return
            if half == 0:
                perms[(c, t)] = permp.tile([P, 1024], F32, name="perm", tag="perm")
            for g in (2 * half, 2 * half + 1):
                src = raws[c][:, t * 1024 + 256 * g:t * 1024 + 256 * (g + 1)]
                nc.scalar.copy(
                    out=perms[(c, t)][:, 256 * g:256 * (g + 1)].rearrange("p (u k i) -> p k u i", u=2, i=4),
                    in_=src.rearrange("p (k i u) -> p k u i", i=4, u=2),
                )

        def words_of(c, t, g, u):
            if (c, t) in perms:
                start = 256 * g + 128 * u
                return perms[(c, t)][:, start:start + P]
            start = t * 1024 + 256 * g + u
            return raws[c][:, start:start + 2 * P - 1:2]

        def transpose_bank(sources):
            bank = tps.tile([P, 512], F32, name="tbank", tag="tbank")
            for j in range(4):
                nc.tensor.transpose(out=bank[:, j * P:(j + 1) * P], in_=sources[j], identity=ident[:])
            return bank

        def rows_to_grouped(c, t):
            banks = [transpose_bank([words_of(c, t, 2 * gp + j // 2, j % 2) for j in range(4)]) for gp in range(2)]
            grouped = grp.tile([P, 2048], BF16, name="grouped", tag="grouped", align_bytes=64)
            gw = grouped[:].bitcast(F32)
            for gp in range(2):
                nc.scalar.copy(
                    out=gw[:, gp * 512:(gp + 1) * 512].rearrange("p (g r u) -> p g r u", g=2, u=2),
                    in_=banks[gp][:].rearrange("p (g u r) -> p g r u", g=2, u=2),
                )
            return grouped

        def pass_to_grouped(c, g):
            banks = [transpose_bank([words_of(c, 2 * fp + (j % 2), g, j // 2) for j in range(4)]) for fp in range(2)]
            grouped = grp.tile([P, 2048], BF16, name="grouped", tag="grouped", align_bytes=64)
            gw = grouped[:].bitcast(F32)
            for fp in range(2):
                nc.scalar.copy(
                    out=gw[:, fp * 512:(fp + 1) * 512].rearrange("p (r t u) -> p r t u", t=2, u=2),
                    in_=banks[fp][:].rearrange("p (u t r) -> p r t u", t=2, u=2),
                )
            return grouped

        wq = {}

        def new_wq(c):
            wc = wqp.tile([P, 4 * 512], U32, name="wc", tag="wc", align_bytes=64)
            ws = wqp.tile([P, 4 * 512], U8, name="ws", tag="ws", align_bytes=64)
            wq[c] = (wc, ws)

        def quantise_x(grouped, b):
            cols = slice(b * 512, (b + 1) * 512)
            nc.vector.quantize_mx(out=xc[:, cols].bitcast(FP8X4), scales=xs[:, cols], in_=grouped[:])

        def quantise_pass(grouped, c, g):
            wc, ws = wq[c]
            cols = slice(g * 512, (g + 1) * 512)
            nc.vector.quantize_mx(out=wc[:, cols].bitcast(FP8X4), scales=ws[:, cols], in_=grouped[:])

        def quantise_rows(grouped, c, t):
            wc, ws = wq[c]
            for g in range(4):
                cols = slice(g * 512 + t * P, g * 512 + (t + 1) * P)
                nc.vector.quantize_mx(
                    out=wc[:, cols].bitcast(FP8X4), scales=ws[:, cols], in_=grouped[:, g * 512:(g + 1) * 512]
                )

        def mx_group(c, b):
            acc = accp.tile([P, 512], F32, name="acc", tag="acc")
            wc, ws = wq[c]
            for g in range(4):
                xcols = slice(b * 512 + g * P, b * 512 + (g + 1) * P)
                wcols = slice(g * 512, (g + 1) * 512)
                nc.tensor.matmul_mx(
                    out=acc[:],
                    lhsT=xc[:, xcols].bitcast(FP8X4), lhsT_scale=xs[:, xcols],
                    rhs=wc[:, wcols].bitcast(FP8X4), rhs_scale=ws[:, wcols],
                    start=(g == 0), stop=(g == 3),
                )
            return acc

        deferred = []
        cursor = [0]

        def run_deferred(n):
            for i in range(n):
                if cursor[0] < len(deferred):
                    deferred[cursor[0]]()
                    cursor[0] = cursor[0] + 1

        def store(dram, b, idx, o):
            nc.sync.dma_start(
                out=dram[b, idx * 4:(idx + 1) * 4, :, :].rearrange("h s d -> s h d"),
                in_=o[:].rearrange("p (h d) -> p h d", h=4),
            )

        def evacuate(c, b, acc):
            is_key, idx = CHUNKS[c]
            bias = biases[c]
            if not is_key:
                o = outp.tile([P, 512], F32, name="o", tag="o")
                nc.vector.tensor_tensor(out=o[:], in0=acc[:], in1=bias[:], op=ADD)
                store(out_1, b, idx, o)
                return
            pb = tmpp.tile([P, 512], F32, name="pb", tag="pb")
            nc.vector.tensor_tensor(out=pb[:], in0=acc[:], in1=bias[:], op=ADD)
            held = {}

            def mul_sin():
                t2 = tmpp.tile([P, 512], F32, name="t2", tag="t2")
                nc.vector.tensor_tensor(
                    out=t2[:].rearrange("p (h a i) -> p h a i", h=4, a=2),
                    in0=pb[:].rearrange("p (h a i) -> p h a i", h=4, a=2)[:, :, ::-1, :],
                    in1=sin_b.rearrange("p h (a i) -> p h a i", a=2), op=MULT,
                )
                held["t2"] = t2

            def mul_cos():
                o = outp.tile([P, 512], F32, name="o", tag="o")
                nc.vector.tensor_tensor(
                    out=o[:].rearrange("p (h d) -> p h d", h=4), in0=pb[:].rearrange("p (h d) -> p h d", h=4),
                    in1=cos_b, op=MULT,
                )
                held["o"] = o

            def combine():
                o = held["o"]
                last_key = (idx, b) == (3, B - 1)
                pieces = 2 if last_key else 1
                heads = 4 // pieces
                for i in range(pieces):
                    part = slice(i * heads * HD, (i + 1) * heads * HD)
                    nc.vector.tensor_tensor(out=o[:, part], in0=o[:, part], in1=held["t2"][:, part], op=ADD)
                    nc.sync.dma_start(
                        out=out_0[b, idx * 4 + i * heads:idx * 4 + (i + 1) * heads, :, :].rearrange("h s d -> s h d"),
                        in_=o[:, part].rearrange("p (h d) -> p h d", d=HD),
                    )

            deferred.extend([mul_cos, mul_sin, combine])

        warm_bank = accp.tile([P, 512], F32, name="acc", tag="acc")

        def keep_warm(n):
            for i in range(n):
                nc.tensor.matmul(out=warm_bank[:], lhsT=zeros[:, 0:P], rhs=zeros[:], start=True, stop=True)

        new_wq(0)
        gx = {}
        gw = {}
        keep_warm(5)
        gx[0] = rows_to_grouped("x", 0)
        keep_warm(1)
        gw[0] = rows_to_grouped(0, 0)
        quantise_x(gx[0], 0)
        keep_warm(1)
        gw[1] = rows_to_grouped(0, 1)
        quantise_rows(gw[0], 0, 0)
        bias_table(0, False)
        gw[2] = rows_to_grouped(0, 2)
        quantise_rows(gw[1], 0, 1)
        bias_table(1, False)
        gw[3] = rows_to_grouped(0, 3)
        quantise_rows(gw[2], 0, 2)
        rope_tables()
        keep_warm(1)
        gx[1] = rows_to_grouped("x", 1)
        quantise_rows(gw[3], 0, 3)
        keep_warm(1)
        gx[2] = rows_to_grouped("x", 2)
        quantise_x(gx[1], 1)
        acc = mx_group(0, 0)
        gx[3] = rows_to_grouped("x", 3)
        evacuate(0, 0, acc)
        quantise_x(gx[2], 2)
        acc = mx_group(0, 1)
        run_deferred(1)
        evacuate(0, 1, acc)
        quantise_x(gx[3], 3)
        acc = mx_group(0, 2)
        new_wq(1)
        g0 = pass_to_grouped(1, 0)
        run_deferred(2)
        evacuate(0, 2, acc)
        quantise_pass(g0, 1, 0)
        acc = mx_group(0, 3)
        g1 = pass_to_grouped(1, 1)
        run_deferred(1)
        evacuate(0, 3, acc)
        quantise_pass(g1, 1, 1)
        g2 = pass_to_grouped(1, 2)
        g3 = pass_to_grouped(1, 3)
        run_deferred(2)
        quantise_pass(g2, 1, 2)
        run_deferred(1)
        quantise_pass(g3, 1, 3)

        for c in range(1, LAST + 1):
            more = c < LAST
            if c + 4 <= LAST:
                load_by_row_pairs(c + 4)
            for half in range(2):
                if more:
                    if half == 0:
                        new_wq(c + 1)
                    ga = pass_to_grouped(c + 1, 2 * half)
                    permute(c + 2, 2 * half)
                acc_a = mx_group(c, 2 * half)
                if more:
                    gb = pass_to_grouped(c + 1, 2 * half + 1)
                    permute(c + 2, 2 * half + 1)
                acc_b = mx_group(c, 2 * half + 1)
                run_deferred(DEFER_A)
                if more:
                    quantise_pass(ga, c + 1, 2 * half)
                run_deferred(DEFER_B)
                evacuate(c, 2 * half, acc_a)
                if more:
                    quantise_pass(gb, c + 1, 2 * half + 1)
                evacuate(c, 2 * half + 1, acc_b)
            bias_table(c + 1, True)
        run_deferred(len(deferred))
